import numpy as np
import ml_dtypes

BF16 = ml_dtypes.bfloat16


def bf(x):
    return np.asarray(x, np.float32).astype(BF16)


def f32(x):
    return np.asarray(x, np.float32)


def f64(x):
    return np.asarray(x).astype(np.float64)


def striped(idx):
    return np.tile(idx.reshape(-1, 16).T, (8, 1))


C, S, N = 512, 2048, 256


def setup_inputs():
    return {"k_cache": f32(np.random.standard_normal((C, S))), "k_new": f32(np.random.standard_normal((C, N))), "offs": striped(np.random.permutation(S)[:N])}


def reference(k_cache, k_new, offs):
    idx = offs[:16].T.reshape(-1)
    res = f64(k_cache).copy()
    res[:, idx] = f64(k_new)
    return res

@@ -1,0 +1,30 @@
+import concourse.mybir as mybir
+
+F32 = mybir.dt.float32
+U16 = mybir.dt.uint16
+COPY = mybir.ActivationFunctionType.Copy
+
+P = 128
+CHANNELS, SLOTS, TOKENS = 512, 2048, 256
+BLOCKS = CHANNELS // P
+
+BYTES = 4 * CHANNELS * (SLOTS + (SLOTS - TOKENS) + TOKENS) + 2 * P * (TOKENS // 16)
+
+
+def tile_blockattention_kernel(tc, k_cache, k_new, offs, out):
+    nc = tc.nc
+    with (
+        tc.tile_pool(name="held", bufs=1) as held,
+        tc.tile_pool(name="blocks", bufs=BLOCKS) as blocks,
+    ):
+        offsets = held.tile([P, TOKENS // 16], U16, name="offsets")
+        nc.sync.dma_start(offsets[:], offs)
+
+        for b in range(BLOCKS):
+            rows = slice(b * P, (b + 1) * P)
+            tokens = blocks.tile([P, TOKENS], F32, name="tokens")
+            window = blocks.tile([P, SLOTS], F32, name="window")
+            nc.sync.dma_start(tokens[:], k_new[rows, :])
+            nc.sync.dma_start(window[:], k_cache[rows, :])
+            nc.scalar.activation(window[:].indirect(offsets[:]), tokens[:], COPY)
+            nc.scalar.dma_start(out[rows, :], window[:])

@@ -20,11 +20,16 @@ def tile_blockattention_kernel(tc, k_cache, k_new, offs, out):
         offsets = held.tile([P, TOKENS // 16], U16, name="offsets")
         nc.sync.dma_start(offsets[:], offs)
 
+        tokens = []
+        windows = []
         for b in range(BLOCKS):
             rows = slice(b * P, (b + 1) * P)
-            tokens = blocks.tile([P, TOKENS], F32, name="tokens")
-            window = blocks.tile([P, SLOTS], F32, name="window")
-            nc.sync.dma_start(tokens[:], k_new[rows, :])
-            nc.sync.dma_start(window[:], k_cache[rows, :])
-            nc.scalar.activation(window[:].indirect(offsets[:]), tokens[:], COPY)
-            nc.scalar.dma_start(out[rows, :], window[:])
+            tokens.append(blocks.tile([P, TOKENS], F32, name="tokens"))
+            windows.append(blocks.tile([P, SLOTS], F32, name="window"))
+            nc.sync.dma_start(tokens[b][:], k_new[rows, :])
+            nc.sync.dma_start(windows[b][:], k_cache[rows, :])
+
+        for b in range(BLOCKS):
+            rows = slice(b * P, (b + 1) * P)
+            nc.scalar.activation(windows[b][:].indirect(offsets[:]), tokens[b][:], COPY)
+            nc.sync.dma_start(out[rows, :], windows[b][:])

@@ -13,23 +13,21 @@ BYTES = 4 * CHANNELS * (SLOTS + (SLOTS - TOKENS) + TOKENS) + 2 * P * (TOKENS // 
 
 def tile_blockattention_kernel(tc, k_cache, k_new, offs, out):
     nc = tc.nc
+    cache_blocks = k_cache.rearrange("(p b) s -> b p s", b=BLOCKS)
+    out_blocks = out.rearrange("(p b) s -> b p s", b=BLOCKS)
     with (
         tc.tile_pool(name="held", bufs=1) as held,
         tc.tile_pool(name="blocks", bufs=BLOCKS) as blocks,
     ):
         offsets = held.tile([P, TOKENS // 16], U16, name="offsets")
         nc.sync.dma_start(offsets[:], offs)
-
-        tokens = []
-        windows = []
-        for b in range(BLOCKS):
-            rows = slice(b * P, (b + 1) * P)
-            tokens.append(blocks.tile([P, TOKENS], F32, name="tokens"))
-            windows.append(blocks.tile([P, SLOTS], F32, name="window"))
-            nc.sync.dma_start(tokens[b][:], k_new[rows, :])
-            nc.sync.dma_start(windows[b][:], k_cache[rows, :])
+        tokens = held.tile([P, BLOCKS * TOKENS], F32, name="tokens")
+        nc.sync.dma_start(tokens[:], k_new.rearrange("(p b) n -> p (b n)", b=BLOCKS))
 
         for b in range(BLOCKS):
-            rows = slice(b * P, (b + 1) * P)
-            nc.scalar.activation(windows[b][:].indirect(offsets[:]), tokens[b][:], COPY)
-            nc.sync.dma_start(out[rows, :], windows[b][:])
+            window = blocks.tile([P, SLOTS], F32, name="window")
+            nc.sync.dma_start(window[:], cache_blocks[b])
+            nc.scalar.activation(
+                window[:].indirect(offsets[:]), tokens[:, b * TOKENS : (b + 1) * TOKENS], COPY
+            )
+            nc.scalar.dma_start(out_blocks[b], window[:])

@@ -7,6 +7,7 @@ COPY = mybir.ActivationFunctionType.Copy
 P = 128
 CHANNELS, SLOTS, TOKENS = 512, 2048, 256
 BLOCKS = CHANNELS // P
+ROW_ALIGN_BYTES = 4096
 
 BYTES = 4 * CHANNELS * (SLOTS + (SLOTS - TOKENS) + TOKENS) + 2 * P * (TOKENS // 16)
 
@@ -21,11 +22,11 @@ def tile_blockattention_kernel(tc, k_cache, k_new, offs, out):
     ):
         offsets = held.tile([P, TOKENS // 16], U16, name="offsets")
         nc.sync.dma_start(offsets[:], offs)
-        tokens = held.tile([P, BLOCKS * TOKENS], F32, name="tokens")
+        tokens = held.tile([P, BLOCKS * TOKENS], F32, name="tokens", align_bytes=ROW_ALIGN_BYTES)
         nc.sync.dma_start(tokens[:], k_new.rearrange("(p b) n -> p (b n)", b=BLOCKS))
 
         for b in range(BLOCKS):
-            window = blocks.tile([P, SLOTS], F32, name="window")
+            window = blocks.tile([P, SLOTS], F32, name="window", align_bytes=ROW_ALIGN_BYTES)
             nc.sync.dma_start(window[:], cache_blocks[b])
             nc.scalar.activation(
                 window[:].indirect(offsets[:]), tokens[:, b * TOKENS : (b + 1) * TOKENS], COPY

@@ -20,10 +20,10 @@ def tile_blockattention_kernel(tc, k_cache, k_new, offs, out):
         tc.tile_pool(name="held", bufs=1) as held,
         tc.tile_pool(name="blocks", bufs=BLOCKS) as blocks,
     ):
-        offsets = held.tile([P, TOKENS // 16], U16, name="offsets")
-        nc.sync.dma_start(offsets[:], offs)
         tokens = held.tile([P, BLOCKS * TOKENS], F32, name="tokens", align_bytes=ROW_ALIGN_BYTES)
         nc.sync.dma_start(tokens[:], k_new.rearrange("(p b) n -> p (b n)", b=BLOCKS))
+        offsets = held.tile([P, TOKENS // 16], U16, name="offsets")
+        nc.sync.dma_start(offsets[:], offs)
 
         for b in range(BLOCKS):
             window = blocks.tile([P, SLOTS], F32, name="window", align_bytes=ROW_ALIGN_BYTES)

@@ -25,10 +25,15 @@ def tile_blockattention_kernel(tc, k_cache, k_new, offs, out):
         offsets = held.tile([P, TOKENS // 16], U16, name="offsets")
         nc.sync.dma_start(offsets[:], offs)
 
+        windows = []
         for b in range(BLOCKS):
             window = blocks.tile([P, SLOTS], F32, name="window", align_bytes=ROW_ALIGN_BYTES)
             nc.sync.dma_start(window[:], cache_blocks[b])
+            windows.append(window)
+
+        for b in range(BLOCKS):
             nc.scalar.activation(
-                window[:].indirect(offsets[:]), tokens[:, b * TOKENS : (b + 1) * TOKENS], COPY
+                windows[b][:].indirect(offsets[:]), tokens[:, b * TOKENS : (b + 1) * TOKENS], COPY
             )
-            nc.scalar.dma_start(out_blocks[b], window[:])
+            store_queue = nc.scalar if b % 2 == 0 else nc.sync
+            store_queue.dma_start(out_blocks[b], windows[b][:])

@@ -35,5 +35,10 @@ def tile_blockattention_kernel(tc, k_cache, k_new, offs, out):
             nc.scalar.activation(
                 windows[b][:].indirect(offsets[:]), tokens[:, b * TOKENS : (b + 1) * TOKENS], COPY
             )
-            store_queue = nc.scalar if b % 2 == 0 else nc.sync
+            if b == 0:
+                store_queue = nc.scalar
+            elif b < BLOCKS - 1:
+                store_queue = nc.gpsimd
+            else:
+                store_queue = nc.sync
             store_queue.dma_start(out_blocks[b], windows[b][:])

@@ -21,15 +21,16 @@ def tile_blockattention_kernel(tc, k_cache, k_new, offs, out):
         tc.tile_pool(name="blocks", bufs=BLOCKS) as blocks,
     ):
         tokens = held.tile([P, BLOCKS * TOKENS], F32, name="tokens", align_bytes=ROW_ALIGN_BYTES)
-        nc.sync.dma_start(tokens[:], k_new.rearrange("(p b) n -> p (b n)", b=BLOCKS))
+        nc.scalar.dma_start(tokens[:], k_new.rearrange("(p b) n -> p (b n)", b=BLOCKS))
         offsets = held.tile([P, TOKENS // 16], U16, name="offsets")
-        nc.sync.dma_start(offsets[:], offs)
 
         windows = []
         for b in range(BLOCKS):
             window = blocks.tile([P, SLOTS], F32, name="window", align_bytes=ROW_ALIGN_BYTES)
             nc.sync.dma_start(window[:], cache_blocks[b])
             windows.append(window)
+            if b == 0:
+                nc.sync.dma_start(offsets[:], offs)
 
         for b in range(BLOCKS):
             nc.scalar.activation(

@@ -24,6 +24,11 @@ def tile_blockattention_kernel(tc, k_cache, k_new, offs, out):
         nc.scalar.dma_start(tokens[:], k_new.rearrange("(p b) n -> p (b n)", b=BLOCKS))
         offsets = held.tile([P, TOKENS // 16], U16, name="offsets")
 
+        zeros = held.tile([P, 1], F32, name="zeros")
+        copied_zeros = held.tile([P, 1], F32, name="copied_zeros")
+        nc.vector.memset(zeros[:], 0.0)
+        nc.scalar.activation(copied_zeros[:], zeros[:], COPY)
+
         windows = []
         for b in range(BLOCKS):
             window = blocks.tile([P, SLOTS], F32, name="window", align_bytes=ROW_ALIGN_BYTES)

@@ -41,10 +41,5 @@ def tile_blockattention_kernel(tc, k_cache, k_new, offs, out):
             nc.scalar.activation(
                 windows[b][:].indirect(offsets[:]), tokens[:, b * TOKENS : (b + 1) * TOKENS], COPY
             )
-            if b == 0:
-                store_queue = nc.scalar
-            elif b < BLOCKS - 1:
-                store_queue = nc.gpsimd
-            else:
-                store_queue = nc.sync
+            store_queue = nc.gpsimd if b < BLOCKS // 2 else nc.sync
             store_queue.dma_start(out_blocks[b], windows[b][:])

import concourse.mybir as mybir

F32 = mybir.dt.float32
U16 = mybir.dt.uint16
COPY = mybir.ActivationFunctionType.Copy

P = 128
CHANNELS, SLOTS, TOKENS = 512, 2048, 256
BLOCKS = CHANNELS // P
ROW_ALIGN_BYTES = 4096

BYTES = 4 * CHANNELS * (SLOTS + (SLOTS - TOKENS) + TOKENS) + 2 * P * (TOKENS // 16)


def tile_blockattention_kernel(tc, k_cache, k_new, offs, out):
    nc = tc.nc
    cache_blocks = k_cache.rearrange("(p b) s -> b p s", b=BLOCKS)
    out_blocks = out.rearrange("(p b) s -> b p s", b=BLOCKS)
    with (
        tc.tile_pool(name="held", bufs=1) as held,
        tc.tile_pool(name="blocks", bufs=BLOCKS) as blocks,
    ):
        tokens = held.tile([P, BLOCKS * TOKENS], F32, name="tokens", align_bytes=ROW_ALIGN_BYTES)
        nc.scalar.dma_start(tokens[:], k_new.rearrange("(p b) n -> p (b n)", b=BLOCKS))
        offsets = held.tile([P, TOKENS // 16], U16, name="offsets")

        zeros = held.tile([P, 1], F32, name="zeros")
        copied_zeros = held.tile([P, 1], F32, name="copied_zeros")
        nc.vector.memset(zeros[:], 0.0)
        nc.scalar.activation(copied_zeros[:], zeros[:], COPY)

        windows = []
        for b in range(BLOCKS):
            window = blocks.tile([P, SLOTS], F32, name="window", align_bytes=ROW_ALIGN_BYTES)
            nc.sync.dma_start(window[:], cache_blocks[b])
            windows.append(window)
            if b == 0:
                nc.sync.dma_start(offsets[:], offs)

        for b in range(BLOCKS):
            nc.scalar.activation(
                windows[b][:].indirect(offsets[:]), tokens[:, b * TOKENS : (b + 1) * TOKENS], COPY
            )
            store_queue = nc.gpsimd if b < BLOCKS // 2 else nc.sync
            store_queue.dma_start(out_blocks[b], windows[b][:])
